import numpy as np
import ml_dtypes


def mxq(x, axis, fmt="e4m3"):
    dtype, down = {"e4m3": (ml_dtypes.float8_e4m3fn, 7), "e5m2": (ml_dtypes.float8_e5m2, 14)}[fmt]
    v = np.moveaxis(np.asarray(x, np.float32).astype(ml_dtypes.bfloat16).astype(np.float64), axis, -1)
    blocks = v.reshape(v.shape[:-1] + (-1, 32))
    amax = np.abs(blocks).max(-1, keepdims=True)
    byte = np.maximum(np.where(amax > 0, np.frexp(amax)[1] - 1 + 127, 0) - down, 1)
    scale = np.exp2(byte - 127.0)
    codes = (blocks / scale).astype(np.float32).astype(dtype).astype(np.float64)
    return np.moveaxis((codes * scale).reshape(v.shape), -1, axis)


WIDE = False


def mx_kscale(k):
    if not WIDE:
        return np.ones(k)
    levels = np.array([10, -10, 5, -5, 0])
    if k % 512:
        return np.exp2(np.random.permutation(np.resize(levels, k // 32))).repeat(32)
    a = np.empty((k // 512, 16))
    for p in range(k // 512):
        a[p, :8] = np.random.permutation(np.resize(levels, 8))
        for g in range(8):
            far = levels[np.abs(levels - a[p, g]) >= 10]
            a[p, g + 8] = far[np.random.randint(len(far))]
    return np.exp2(a.ravel()).repeat(32)


BF16 = ml_dtypes.bfloat16


def bf(x):
    return np.asarray(x, np.float32).astype(BF16)


def f64(x):
    return np.asarray(x).astype(np.float64)


B, N, NFEAT, NHID, NHID2, NCLASS = 2, 1024, 512, 512, 1024, 256


def setup_inputs():
    t, s = mx_kscale(NFEAT), mx_kscale(N)
    return {"x": bf(np.random.standard_normal((B, N, NFEAT)) * t / s[:, None]),
            "adj": bf(np.random.uniform(size=(N, N)) * s),
            "S": bf(np.random.standard_normal((N, N)) * 1.7 / np.sqrt(N)),
            "W1": bf(np.random.standard_normal((NFEAT, NHID)) / np.sqrt(NFEAT) / t[:, None])}


def reference(x, adj, S, W1):
    support = mxq(f64(x), 2, "e4m3") @ mxq(f64(W1), 0, "e4m3")
    weighting = f64(adj) * f64(S)
    out = mxq(weighting, 1, "e4m3") @ mxq(support, 1, "e4m3")
    return np.maximum(out, 0.0)

@@ -1,0 +1,237 @@
+from contextlib import ExitStack
+
+import concourse.mybir as mybir
+from concourse.masks import make_identity
+
+BF16 = mybir.dt.bfloat16
+F32 = mybir.dt.float32
+U32 = mybir.dt.uint32
+U8 = mybir.dt.uint8
+FP8X4 = mybir.dt.float8_e4m3fn_x4
+
+P = 128
+PACK = 4
+K_PASS = P * PACK
+
+BATCH = 2
+NODES = 1024
+FEATURES = 512
+HIDDEN = 512
+NODE_PASSES = NODES // K_PASS
+HALVES = BATCH * NODE_PASSES
+NODE_TILES = NODES // P
+PAIRS = NODE_TILES // 2
+QUARTERS = HIDDEN // P
+
+FLOPS = 2 * BATCH * NODES * FEATURES * HIDDEN + 2 * BATCH * NODES * NODES * HIDDEN
+
+
+def tile_gcn_pa_kernel(tc, x, adj, S, W1, out):
+    nc = tc.nc
+
+    with ExitStack() as ctx:
+        ctx.enter_context(tc.manual_schedule())
+        keep = ctx.enter_context(tc.tile_pool(name="keep", bufs=1))
+        tr_psum = ctx.enter_context(tc.psum_pool(name="tr_psum", bufs=4))
+        mm_psum = ctx.enter_context(tc.psum_pool(name="mm_psum", bufs=4))
+
+        w1_rows = keep.tile([P, PACK, HIDDEN], BF16, name="w1_rows")
+        nc.sync.dma_start(
+            out=w1_rows[:],
+            in_=W1.rearrange("(q t) h -> q t h", t=PACK),
+        )
+        x_view = x.rearrange("b (g p u e) k -> b g p u e k", g=NODE_PASSES, u=2, e=2)
+        x_rows = {}
+        for i in range(HALVES):
+            for u in range(2):
+                x_rows[(i, u)] = keep.tile([P, 2, FEATURES], BF16, name="x_rows%d_%d" % (i, u))
+                nc.sync.dma_start(out=x_rows[(i, u)][:], in_=x_view[i // NODE_PASSES, i % NODE_PASSES, :, u])
+        adj_view = adj.rearrange("(p t) m -> p t m", t=NODE_TILES)
+        s_view = S.rearrange("(p t) m -> p t m", t=NODE_TILES)
+        out_view = out.rearrange("b (p t) h -> b p t h", t=NODE_TILES)
+        adj_rows = []
+        s_rows = []
+        for r in range(PAIRS):
+            a = keep.tile([P, 2, NODES], BF16, name="adj_rows%d" % r)
+            nc.sync.dma_start(out=a[:], in_=adj_view[:, 2 * r : 2 * r + 2, :])
+            adj_rows.append(a)
+            s = keep.tile([P, 2, NODES], BF16, name="s_rows%d" % r)
+            nc.sync.dma_start(out=s[:], in_=s_view[:, 2 * r : 2 * r + 2, :])
+            s_rows.append(s)
+
+        ident = keep.tile([P, P], F32, name="ident")
+        make_identity(nc, ident[:])
+
+        w1_grouped = keep.tile([P, HIDDEN, PACK], BF16, name="w1_grouped", align_bytes=64)
+        nc.vector.tensor_copy(
+            out=w1_grouped[:].rearrange("q (c i) t -> q c t i", i=4),
+            in_=w1_rows[:].rearrange("q t (c i) -> q c t i", i=4),
+        )
+        w1_codes = keep.tile([P, HIDDEN], U32, name="w1_codes", align_bytes=64)
+        w1_scales = keep.tile([P, HIDDEN], U8, name="w1_scales", align_bytes=64)
+        nc.vector.quantize_mx(
+            out=w1_codes[:].bitcast(FP8X4),
+            scales=w1_scales[:],
+            in_=w1_grouped[:].rearrange("q h t -> q (h t)"),
+        )
+
+        def quantise(name, grouped):
+            codes = keep.tile([P, K_PASS], U32, name=name + "_codes", align_bytes=64)
+            scales = keep.tile([P, K_PASS], U8, name=name + "_scales", align_bytes=64)
+            nc.vector.quantize_mx(out=codes[:].bitcast(FP8X4), scales=scales[:], in_=grouped)
+            return codes, scales
+
+        def transpose_words(rows):
+            bank = tr_psum.tile([P, PACK, P], F32, tag="tr", name="tr_bank")
+            for c in range(PACK):
+                first = (c // 2) * 2 * P + c % 2
+                nc.tensor.transpose(bank[:, c, :], rows[:, first : first + 2 * P - 1 : 2], ident[:])
+            return bank
+
+        x_banks = {}
+        x_grouped = {}
+        x_q = {}
+        sup_banks = {}
+        sup_grouped = {}
+        sup_q = {}
+
+        def transpose_x(i):
+            x_banks[i] = [
+                transpose_words(x_rows[(i, u)][:].bitcast(F32).rearrange("p e w -> p (e w)")) for u in range(2)
+            ]
+
+        def copy_x(i):
+            x_grouped[i] = keep.tile([P, PACK, P, PACK], BF16, name="x_grouped%d" % i, align_bytes=64)
+            for u in range(2):
+                nc.scalar.copy(
+                    out=x_grouped[i][:, 2 * u : 2 * u + 2, :, :].bitcast(F32),
+                    in_=x_banks[i][u][:].rearrange("q (e uk) m -> q e m uk", e=2),
+                )
+
+        def quantise_x(i):
+            x_q[i] = quantise("x%d" % i, x_grouped[i][:].rearrange("q j m t -> q (j m t)"))
+
+        def support_matmuls(i):
+            codes, scales = x_q[i]
+            sup_banks[i] = []
+            for hq in range(QUARTERS):
+                h_cols = slice(hq * P, (hq + 1) * P)
+                bank = mm_psum.tile([P, PACK, P], F32, tag="mm", name="sup_bank")
+                for j in range(PACK):
+                    m_cols = slice(j * P, (j + 1) * P)
+                    nc.tensor.matmul_mx(
+                        out=bank[:, j, :],
+                        lhsT=codes[:, m_cols].bitcast(FP8X4),
+                        lhsT_scale=scales[:, m_cols],
+                        rhs=w1_codes[:, h_cols].bitcast(FP8X4),
+                        rhs_scale=w1_scales[:, h_cols],
+                        start=True,
+                        stop=True,
+                    )
+                sup_banks[i].append(bank)
+
+        def copy_support(i):
+            sup_grouped[i] = keep.tile([P, HIDDEN, PACK], BF16, name="sup_grouped%d" % i, align_bytes=64)
+            first_on_vector = 2 if i < NODE_PASSES else 3
+            for hq in range(QUARTERS):
+                dst = sup_grouped[i][:, hq * P : (hq + 1) * P, :]
+                src = sup_banks[i][hq][:].rearrange("p j h -> p h j")
+                if hq >= first_on_vector:
+                    nc.vector.tensor_copy(out=dst, in_=src)
+                else:
+                    nc.scalar.copy(out=dst, in_=src)
+
+        def quantise_support(i):
+            sup_q[i] = quantise("sup%d" % i, sup_grouped[i][:].rearrange("p h j -> p (h j)"))
+
+        w_rows = {}
+        w_banks = {}
+        w_grouped = {}
+        w_q = {}
+        out_banks = {}
+
+        def product(r):
+            w_rows[r] = keep.tile([P, 2, NODES], BF16, name="w_rows%d" % r)
+            nc.vector.tensor_tensor(
+                out=w_rows[r][:], in0=adj_rows[r][:], in1=s_rows[r][:], op=mybir.AluOpType.mult
+            )
+
+        def transpose_w(r):
+            words = w_rows[r][:].bitcast(F32)
+            w_banks[r] = [transpose_words(words[:, t, :]) for t in range(2)]
+
+        def copy_w(r):
+            w_grouped[r] = keep.tile([P, 2, NODE_PASSES, P, PACK], BF16, name="w_grouped%d" % r, align_bytes=64)
+            for t in range(2):
+                nc.scalar.copy(
+                    out=w_grouped[r][:, t, :, :, :].bitcast(F32),
+                    in_=w_banks[r][t][:].rearrange("p (g u) n -> p g n u", g=NODE_PASSES),
+                )
+
+        def quantise_w(r):
+            w_q[r] = quantise("w%d" % r, w_grouped[r][:].rearrange("p t g n v -> p (t g n v)"))
+
+        def output_matmuls(r):
+            codes, scales = w_q[r]
+            for b in range(BATCH):
+                for t in range(2):
+                    bank = mm_psum.tile([P, HIDDEN], F32, tag="mm", name="out_bank")
+                    for g in range(NODE_PASSES):
+                        n_cols = slice((t * NODE_PASSES + g) * P, (t * NODE_PASSES + g + 1) * P)
+                        s_codes, s_scales = sup_q[b * NODE_PASSES + g]
+                        nc.tensor.matmul_mx(
+                            out=bank[:],
+                            lhsT=codes[:, n_cols].bitcast(FP8X4),
+                            lhsT_scale=scales[:, n_cols],
+                            rhs=s_codes[:].bitcast(FP8X4),
+                            rhs_scale=s_scales[:],
+                            start=(g == 0),
+                            stop=(g == NODE_PASSES - 1),
+                        )
+                    out_banks[(r, b, t)] = bank
+
+        def relu_and_store(r):
+            for b in range(BATCH):
+                for t in range(2):
+                    result = keep.tile([P, HIDDEN], F32, name="result%d_%d_%d" % (r, b, t))
+                    if b == BATCH - 1 and t == 1:
+                        nc.vector.tensor_scalar_max(out=result[:], in0=out_banks[(r, b, t)][:], scalar1=0.0)
+                    else:
+                        nc.scalar.activation(
+                            out=result[:], in_=out_banks[(r, b, t)][:], func=mybir.ActivationFunctionType.Relu
+                        )
+                    nc.sync.dma_start(out=out_view[b, :, 2 * r + t, :], in_=result[:])
+
+        transpose_x(0)
+        copy_x(0)
+        transpose_x(1)
+        copy_x(1)
+        quantise_x(0)
+        for i in range(HALVES):
+            support_matmuls(i)
+            if i + 1 < HALVES:
+                quantise_x(i + 1)
+            if i + 2 < HALVES:
+                transpose_x(i + 2)
+            if i == HALVES - 1:
+                transpose_w(0)
+            copy_support(i)
+            if i + 2 < HALVES:
+                copy_x(i + 2)
+            else:
+                product(i + 2 - HALVES)
+            if i == HALVES - 1:
+                copy_w(0)
+            quantise_support(i)
+        quantise_w(0)
+        for r in range(PAIRS):
+            if r + 1 < PAIRS:
+                transpose_w(r + 1)
+            output_matmuls(r)
+            if r + 1 < PAIRS:
+                copy_w(r + 1)
+            if r + 2 < PAIRS:
+                product(r + 2)
+            if r + 1 < PAIRS:
+                quantise_w(r + 1)
+            relu_and_store(r)

@@ -36,13 +36,11 @@ def tile_gcn_pa_kernel(tc, x, adj, S, W1, out):
         mm_psum = ctx.enter_context(tc.psum_pool(name="mm_psum", bufs=4))
 
         w1_rows = keep.tile([P, PACK, HIDDEN], BF16, name="w1_rows")
-        nc.sync.dma_start(
-            out=w1_rows[:],
-            in_=W1.rearrange("(q t) h -> q t h", t=PACK),
-        )
         x_view = x.rearrange("b (g p u e) k -> b g p u e k", g=NODE_PASSES, u=2, e=2)
         x_rows = {}
         for i in range(HALVES):
+            if i == 1:
+                nc.sync.dma_start(out=w1_rows[:], in_=W1.rearrange("(q t) h -> q t h", t=PACK))
             for u in range(2):
                 x_rows[(i, u)] = keep.tile([P, 2, FEATURES], BF16, name="x_rows%d_%d" % (i, u))
                 nc.sync.dma_start(out=x_rows[(i, u)][:], in_=x_view[i // NODE_PASSES, i % NODE_PASSES, :, u])
@@ -63,17 +61,21 @@ def tile_gcn_pa_kernel(tc, x, adj, S, W1, out):
         make_identity(nc, ident[:])
 
         w1_grouped = keep.tile([P, HIDDEN, PACK], BF16, name="w1_grouped", align_bytes=64)
-        nc.vector.tensor_copy(
-            out=w1_grouped[:].rearrange("q (c i) t -> q c t i", i=4),
-            in_=w1_rows[:].rearrange("q t (c i) -> q c t i", i=4),
-        )
         w1_codes = keep.tile([P, HIDDEN], U32, name="w1_codes", align_bytes=64)
         w1_scales = keep.tile([P, HIDDEN], U8, name="w1_scales", align_bytes=64)
-        nc.vector.quantize_mx(
-            out=w1_codes[:].bitcast(FP8X4),
-            scales=w1_scales[:],
-            in_=w1_grouped[:].rearrange("q h t -> q (h t)"),
-        )
+
+        def regroup_w1():
+            nc.vector.tensor_copy(
+                out=w1_grouped[:].rearrange("q (c i) t -> q c t i", i=4),
+                in_=w1_rows[:].rearrange("q t (c i) -> q c t i", i=4),
+            )
+
+        def quantise_w1():
+            nc.vector.quantize_mx(
+                out=w1_codes[:].bitcast(FP8X4),
+                scales=w1_scales[:],
+                in_=w1_grouped[:].rearrange("q h t -> q (h t)"),
+            )
 
         def quantise(name, grouped):
             codes = keep.tile([P, K_PASS], U32, name=name + "_codes", align_bytes=64)
@@ -81,11 +83,10 @@ def tile_gcn_pa_kernel(tc, x, adj, S, W1, out):
             nc.vector.quantize_mx(out=codes[:].bitcast(FP8X4), scales=scales[:], in_=grouped)
             return codes, scales
 
-        def transpose_words(rows):
+        def transpose_words(blocks):
             bank = tr_psum.tile([P, PACK, P], F32, tag="tr", name="tr_bank")
-            for c in range(PACK):
-                first = (c // 2) * 2 * P + c % 2
-                nc.tensor.transpose(bank[:, c, :], rows[:, first : first + 2 * P - 1 : 2], ident[:])
+            for c, block in enumerate(blocks):
+                nc.tensor.transpose(bank[:, c, :], block, ident[:])
             return bank
 
         x_banks = {}
@@ -96,9 +97,12 @@ def tile_gcn_pa_kernel(tc, x, adj, S, W1, out):
         sup_q = {}
 
         def transpose_x(i):
-            x_banks[i] = [
-                transpose_words(x_rows[(i, u)][:].bitcast(F32).rearrange("p e w -> p (e w)")) for u in range(2)
-            ]
+            x_banks[i] = []
+            for u in range(2):
+                words = x_rows[(i, u)][:].bitcast(F32)
+                x_banks[i].append(
+                    transpose_words([words[:, e, uk : uk + 2 * P - 1 : 2] for e in range(2) for uk in range(2)])
+                )
 
         def copy_x(i):
             x_grouped[i] = keep.tile([P, PACK, P, PACK], BF16, name="x_grouped%d" % i, align_bytes=64)
@@ -132,11 +136,11 @@ def tile_gcn_pa_kernel(tc, x, adj, S, W1, out):
 
         def copy_support(i):
             sup_grouped[i] = keep.tile([P, HIDDEN, PACK], BF16, name="sup_grouped%d" % i, align_bytes=64)
-            first_on_vector = 2 if i < NODE_PASSES else 3
+            on_vector = (1, 3) if i == 0 else (3,)
             for hq in range(QUARTERS):
                 dst = sup_grouped[i][:, hq * P : (hq + 1) * P, :]
                 src = sup_banks[i][hq][:].rearrange("p j h -> p h j")
-                if hq >= first_on_vector:
+                if hq in on_vector:
                     nc.vector.tensor_copy(out=dst, in_=src)
                 else:
                     nc.scalar.copy(out=dst, in_=src)
@@ -151,14 +155,21 @@ def tile_gcn_pa_kernel(tc, x, adj, S, W1, out):
         out_banks = {}
 
         def product(r):
-            w_rows[r] = keep.tile([P, 2, NODES], BF16, name="w_rows%d" % r)
+            w_rows[r] = keep.tile([P, 2, NODES // 2, 2], BF16, name="w_rows%d" % r)
+            pairs = "p t (gq u e) -> p u (t gq) e"
             nc.vector.tensor_tensor(
-                out=w_rows[r][:], in0=adj_rows[r][:], in1=s_rows[r][:], op=mybir.AluOpType.mult
+                out=w_rows[r][:],
+                in0=adj_rows[r][:].rearrange(pairs, u=2, e=2),
+                in1=s_rows[r][:].rearrange(pairs, u=2, e=2),
+                op=mybir.AluOpType.mult,
             )
 
         def transpose_w(r):
-            words = w_rows[r][:].bitcast(F32)
-            w_banks[r] = [transpose_words(words[:, t, :]) for t in range(2)]
+            words = w_rows[r][:].rearrange("p u n e -> p (u n e)").bitcast(F32)
+            w_banks[r] = []
+            for t in range(2):
+                firsts = [(2 * NODE_PASSES * u + NODE_PASSES * t + g) * P for g in range(NODE_PASSES) for u in range(2)]
+                w_banks[r].append(transpose_words([words[:, first : first + P] for first in firsts]))
 
         def copy_w(r):
             w_grouped[r] = keep.tile([P, 2, NODE_PASSES, P, PACK], BF16, name="w_grouped%d" % r, align_bytes=64)
@@ -194,7 +205,7 @@ def tile_gcn_pa_kernel(tc, x, adj, S, W1, out):
             for b in range(BATCH):
                 for t in range(2):
                     result = keep.tile([P, HIDDEN], F32, name="result%d_%d_%d" % (r, b, t))
-                    if b == BATCH - 1 and t == 1:
+                    if t == 1 and (b == BATCH - 1 or r == PAIRS - 1):
                         nc.vector.tensor_scalar_max(out=result[:], in0=out_banks[(r, b, t)][:], scalar1=0.0)
                     else:
                         nc.scalar.activation(
@@ -204,34 +215,42 @@ def tile_gcn_pa_kernel(tc, x, adj, S, W1, out):
 
         transpose_x(0)
         copy_x(0)
+        regroup_w1()
+        quantise_x(0)
+        quantise_w1()
         transpose_x(1)
         copy_x(1)
-        quantise_x(0)
-        for i in range(HALVES):
-            support_matmuls(i)
-            if i + 1 < HALVES:
-                quantise_x(i + 1)
-            if i + 2 < HALVES:
-                transpose_x(i + 2)
-            if i == HALVES - 1:
-                transpose_w(0)
-            copy_support(i)
-            if i + 2 < HALVES:
-                copy_x(i + 2)
-            else:
-                product(i + 2 - HALVES)
-            if i == HALVES - 1:
-                copy_w(0)
-            quantise_support(i)
+        quantise_x(1)
+        transpose_x(2)
+        copy_x(2)
+        support_matmuls(0)
+        copy_support(0)
+        quantise_support(0)
+        quantise_x(2)
+        transpose_x(3)
+        copy_x(3)
+        product(0)
+        support_matmuls(1)
+        copy_support(1)
+        quantise_support(1)
+        quantise_x(3)
+        product(1)
+        support_matmuls(2)
+        copy_support(2)
+        quantise_support(2)
+        transpose_w(0)
+        copy_w(0)
         quantise_w(0)
+        support_matmuls(3)
+        copy_support(3)
+        quantise_support(3)
+        product(2)
         for r in range(PAIRS):
             if r + 1 < PAIRS:
                 transpose_w(r + 1)
-            output_matmuls(r)
-            if r + 1 < PAIRS:
                 copy_w(r + 1)
-            if r + 2 < PAIRS:
-                product(r + 2)
-            if r + 1 < PAIRS:
                 quantise_w(r + 1)
+            output_matmuls(r)
+            if r + 3 < PAIRS:
+                product(r + 3)
             relu_and_store(r)

@@ -64,17 +64,19 @@ def tile_gcn_pa_kernel(tc, x, adj, S, W1, out):
         w1_codes = keep.tile([P, HIDDEN], U32, name="w1_codes", align_bytes=64)
         w1_scales = keep.tile([P, HIDDEN], U8, name="w1_scales", align_bytes=64)
 
-        def regroup_w1():
+        def regroup_w1(half):
+            cols = slice(half * HIDDEN // 2, (half + 1) * HIDDEN // 2)
             nc.vector.tensor_copy(
-                out=w1_grouped[:].rearrange("q (c i) t -> q c t i", i=4),
-                in_=w1_rows[:].rearrange("q t (c i) -> q c t i", i=4),
+                out=w1_grouped[:, cols, :].rearrange("q (c i) t -> q c t i", i=4),
+                in_=w1_rows[:, :, cols].rearrange("q t (c i) -> q c t i", i=4),
             )
 
-        def quantise_w1():
+        def quantise_w1(half):
+            cols = slice(half * HIDDEN // 2, (half + 1) * HIDDEN // 2)
             nc.vector.quantize_mx(
-                out=w1_codes[:].bitcast(FP8X4),
-                scales=w1_scales[:],
-                in_=w1_grouped[:].rearrange("q h t -> q (h t)"),
+                out=w1_codes[:, cols].bitcast(FP8X4),
+                scales=w1_scales[:, cols],
+                in_=w1_grouped[:, cols, :].rearrange("q h t -> q (h t)"),
             )
 
         def quantise(name, grouped):
@@ -136,7 +138,7 @@ def tile_gcn_pa_kernel(tc, x, adj, S, W1, out):
 
         def copy_support(i):
             sup_grouped[i] = keep.tile([P, HIDDEN, PACK], BF16, name="sup_grouped%d" % i, align_bytes=64)
-            on_vector = (1, 3) if i == 0 else (3,)
+            on_vector = {0: (1, 3), 1: (3,)}.get(i, ())
             for hq in range(QUARTERS):
                 dst = sup_grouped[i][:, hq * P : (hq + 1) * P, :]
                 src = sup_banks[i][hq][:].rearrange("p j h -> p h j")
@@ -174,83 +176,102 @@ def tile_gcn_pa_kernel(tc, x, adj, S, W1, out):
         def copy_w(r):
             w_grouped[r] = keep.tile([P, 2, NODE_PASSES, P, PACK], BF16, name="w_grouped%d" % r, align_bytes=64)
             for t in range(2):
-                nc.scalar.copy(
-                    out=w_grouped[r][:, t, :, :, :].bitcast(F32),
-                    in_=w_banks[r][t][:].rearrange("p (g u) n -> p g n u", g=NODE_PASSES),
-                )
+                dst = w_grouped[r][:, t, :, :, :].bitcast(F32)
+                src = w_banks[r][t][:].rearrange("p (g u) n -> p g n u", g=NODE_PASSES)
+                if r > 0 and t == 0:
+                    nc.vector.tensor_copy(out=dst, in_=src)
+                else:
+                    nc.scalar.copy(out=dst, in_=src)
 
         def quantise_w(r):
             w_q[r] = quantise("w%d" % r, w_grouped[r][:].rearrange("p t g n v -> p (t g n v)"))
 
-        def output_matmuls(r):
+        def output_matmuls(r, b):
             codes, scales = w_q[r]
-            for b in range(BATCH):
-                for t in range(2):
-                    bank = mm_psum.tile([P, HIDDEN], F32, tag="mm", name="out_bank")
-                    for g in range(NODE_PASSES):
-                        n_cols = slice((t * NODE_PASSES + g) * P, (t * NODE_PASSES + g + 1) * P)
-                        s_codes, s_scales = sup_q[b * NODE_PASSES + g]
-                        nc.tensor.matmul_mx(
-                            out=bank[:],
-                            lhsT=codes[:, n_cols].bitcast(FP8X4),
-                            lhsT_scale=scales[:, n_cols],
-                            rhs=s_codes[:].bitcast(FP8X4),
-                            rhs_scale=s_scales[:],
-                            start=(g == 0),
-                            stop=(g == NODE_PASSES - 1),
-                        )
-                    out_banks[(r, b, t)] = bank
+            for t in range(2):
+                bank = mm_psum.tile([P, HIDDEN], F32, tag="mm", name="out_bank")
+                for g in range(NODE_PASSES):
+                    n_cols = slice((t * NODE_PASSES + g) * P, (t * NODE_PASSES + g + 1) * P)
+                    s_codes, s_scales = sup_q[b * NODE_PASSES + g]
+                    nc.tensor.matmul_mx(
+                        out=bank[:],
+                        lhsT=codes[:, n_cols].bitcast(FP8X4),
+                        lhsT_scale=scales[:, n_cols],
+                        rhs=s_codes[:].bitcast(FP8X4),
+                        rhs_scale=s_scales[:],
+                        start=(g == 0),
+                        stop=(g == NODE_PASSES - 1),
+                    )
+                out_banks[(r, b, t)] = bank
 
-        def relu_and_store(r):
-            for b in range(BATCH):
-                for t in range(2):
-                    result = keep.tile([P, HIDDEN], F32, name="result%d_%d_%d" % (r, b, t))
-                    if t == 1 and (b == BATCH - 1 or r == PAIRS - 1):
-                        nc.vector.tensor_scalar_max(out=result[:], in0=out_banks[(r, b, t)][:], scalar1=0.0)
-                    else:
-                        nc.scalar.activation(
-                            out=result[:], in_=out_banks[(r, b, t)][:], func=mybir.ActivationFunctionType.Relu
-                        )
-                    nc.sync.dma_start(out=out_view[b, :, 2 * r + t, :], in_=result[:])
+        def relu_and_store(r, b):
+            for t in range(2):
+                result = keep.tile([P, HIDDEN], F32, name="result%d_%d_%d" % (r, b, t))
+                if t == 1 and r >= PAIRS // 2:
+                    nc.vector.tensor_scalar_max(out=result[:], in0=out_banks[(r, b, t)][:], scalar1=0.0)
+                else:
+                    nc.scalar.activation(
+                        out=result[:], in_=out_banks[(r, b, t)][:], func=mybir.ActivationFunctionType.Relu
+                    )
+                nc.sync.dma_start(out=out_view[b, :, 2 * r + t, :], in_=result[:])
 
         transpose_x(0)
         copy_x(0)
-        regroup_w1()
+        regroup_w1(0)
         quantise_x(0)
-        quantise_w1()
+        quantise_w1(0)
+        regroup_w1(1)
+        quantise_w1(1)
         transpose_x(1)
         copy_x(1)
-        quantise_x(1)
         transpose_x(2)
         copy_x(2)
+        quantise_x(1)
         support_matmuls(0)
         copy_support(0)
-        quantise_support(0)
         quantise_x(2)
-        transpose_x(3)
-        copy_x(3)
-        product(0)
         support_matmuls(1)
+        transpose_x(3)
+        product(0)
+        transpose_w(0)
+        quantise_support(0)
         copy_support(1)
-        quantise_support(1)
-        quantise_x(3)
+        copy_x(3)
+        copy_w(0)
         product(1)
         support_matmuls(2)
-        copy_support(2)
-        quantise_support(2)
-        transpose_w(0)
-        copy_w(0)
+        quantise_x(3)
+        transpose_w(1)
         quantise_w(0)
+        copy_support(2)
         support_matmuls(3)
-        copy_support(3)
-        quantise_support(3)
         product(2)
-        for r in range(PAIRS):
-            if r + 1 < PAIRS:
-                transpose_w(r + 1)
-                copy_w(r + 1)
-                quantise_w(r + 1)
-            output_matmuls(r)
-            if r + 3 < PAIRS:
-                product(r + 3)
-            relu_and_store(r)
+        transpose_w(2)
+        quantise_support(1)
+        copy_w(1)
+        copy_support(3)
+        product(3)
+        output_matmuls(0, 0)
+        quantise_w(1)
+        quantise_support(2)
+        transpose_w(3)
+        relu_and_store(0, 0)
+        output_matmuls(1, 0)
+        quantise_support(3)
+        copy_w(2)
+        relu_and_store(1, 0)
+        output_matmuls(0, 1)
+        quantise_w(2)
+        relu_and_store(0, 1)
+        output_matmuls(1, 1)
+        copy_w(3)
+        relu_and_store(1, 1)
+        quantise_w(3)
+        output_matmuls(2, 0)
+        output_matmuls(2, 1)
+        relu_and_store(2, 0)
+        relu_and_store(2, 1)
+        output_matmuls(3, 0)
+        output_matmuls(3, 1)
+        relu_and_store(3, 0)
+        relu_and_store(3, 1)

@@ -36,14 +36,18 @@ def tile_gcn_pa_kernel(tc, x, adj, S, W1, out):
         mm_psum = ctx.enter_context(tc.psum_pool(name="mm_psum", bufs=4))
 
         w1_rows = keep.tile([P, PACK, HIDDEN], BF16, name="w1_rows")
-        x_view = x.rearrange("b (g p u e) k -> b g p u e k", g=NODE_PASSES, u=2, e=2)
+        x_view = x.rearrange("b (g p j) k -> b g p j k", g=NODE_PASSES, j=PACK)
         x_rows = {}
         for i in range(HALVES):
             if i == 1:
                 nc.sync.dma_start(out=w1_rows[:], in_=W1.rearrange("(q t) h -> q t h", t=PACK))
-            for u in range(2):
-                x_rows[(i, u)] = keep.tile([P, 2, FEATURES], BF16, name="x_rows%d_%d" % (i, u))
-                nc.sync.dma_start(out=x_rows[(i, u)][:], in_=x_view[i // NODE_PASSES, i % NODE_PASSES, :, u])
+            x_rows[i] = keep.tile([P, PACK, FEATURES], BF16, name="x_rows%d" % i)
+            step = 2 if i == 0 else PACK
+            for j in range(0, PACK, step):
+                nc.sync.dma_start(
+                    out=x_rows[i][:, j : j + step, :],
+                    in_=x_view[i // NODE_PASSES, i % NODE_PASSES, :, j : j + step, :],
+                )
         adj_view = adj.rearrange("(p t) m -> p t m", t=NODE_TILES)
         s_view = S.rearrange("(p t) m -> p t m", t=NODE_TILES)
         out_view = out.rearrange("b (p t) h -> b p t h", t=NODE_TILES)
@@ -101,7 +105,7 @@ def tile_gcn_pa_kernel(tc, x, adj, S, W1, out):
         def transpose_x(i):
             x_banks[i] = []
             for u in range(2):
-                words = x_rows[(i, u)][:].bitcast(F32)
+                words = x_rows[i][:, 2 * u : 2 * u + 2, :].bitcast(F32)
                 x_banks[i].append(
                     transpose_words([words[:, e, uk : uk + 2 * P - 1 : 2] for e in range(2) for uk in range(2)])
                 )

@@ -64,6 +64,14 @@ def tile_gcn_pa_kernel(tc, x, adj, S, W1, out):
         ident = keep.tile([P, P], F32, name="ident")
         make_identity(nc, ident[:])
 
+        zeros = keep.tile([P, HIDDEN], BF16, name="zeros")
+        nc.vector.memset(zeros[:], 0.0)
+        idle_bank = mm_psum.tile([P, HIDDEN], F32, tag="mm", name="idle_bank")
+
+        def keep_busy(count):
+            for i in range(count):
+                nc.tensor.matmul(out=idle_bank[:], lhsT=zeros[:, :P], rhs=zeros[:], start=True, stop=True)
+
         w1_grouped = keep.tile([P, HIDDEN, PACK], BF16, name="w1_grouped", align_bytes=64)
         w1_codes = keep.tile([P, HIDDEN], U32, name="w1_codes", align_bytes=64)
         w1_scales = keep.tile([P, HIDDEN], U8, name="w1_scales", align_bytes=64)
@@ -219,7 +227,9 @@ def tile_gcn_pa_kernel(tc, x, adj, S, W1, out):
                     )
                 nc.sync.dma_start(out=out_view[b, :, 2 * r + t, :], in_=result[:])
 
+        keep_busy(4)
         transpose_x(0)
+        keep_busy(2)
         copy_x(0)
         regroup_w1(0)
         quantise_x(0)
@@ -227,6 +237,7 @@ def tile_gcn_pa_kernel(tc, x, adj, S, W1, out):
         regroup_w1(1)
         quantise_w1(1)
         transpose_x(1)
+        keep_busy(2)
         copy_x(1)
         transpose_x(2)
         copy_x(2)

@@ -219,7 +219,7 @@ def tile_gcn_pa_kernel(tc, x, adj, S, W1, out):
         def relu_and_store(r, b):
             for t in range(2):
                 result = keep.tile([P, HIDDEN], F32, name="result%d_%d_%d" % (r, b, t))
-                if t == 1 and r >= PAIRS // 2:
+                if t == 1 and r > 0:
                     nc.vector.tensor_scalar_max(out=result[:], in0=out_banks[(r, b, t)][:], scalar1=0.0)
                 else:
                     nc.scalar.activation(

from contextlib import ExitStack

import concourse.mybir as mybir
from concourse.masks import make_identity

BF16 = mybir.dt.bfloat16
F32 = mybir.dt.float32
U32 = mybir.dt.uint32
U8 = mybir.dt.uint8
FP8X4 = mybir.dt.float8_e4m3fn_x4

P = 128
PACK = 4
K_PASS = P * PACK

BATCH = 2
NODES = 1024
FEATURES = 512
HIDDEN = 512
NODE_PASSES = NODES // K_PASS
HALVES = BATCH * NODE_PASSES
NODE_TILES = NODES // P
PAIRS = NODE_TILES // 2
QUARTERS = HIDDEN // P

FLOPS = 2 * BATCH * NODES * FEATURES * HIDDEN + 2 * BATCH * NODES * NODES * HIDDEN


def tile_gcn_pa_kernel(tc, x, adj, S, W1, out):
    nc = tc.nc

    with ExitStack() as ctx:
        ctx.enter_context(tc.manual_schedule())
        keep = ctx.enter_context(tc.tile_pool(name="keep", bufs=1))
        tr_psum = ctx.enter_context(tc.psum_pool(name="tr_psum", bufs=4))
        mm_psum = ctx.enter_context(tc.psum_pool(name="mm_psum", bufs=4))

        w1_rows = keep.tile([P, PACK, HIDDEN], BF16, name="w1_rows")
        x_view = x.rearrange("b (g p j) k -> b g p j k", g=NODE_PASSES, j=PACK)
        x_rows = {}
        for i in range(HALVES):
            if i == 1:
                nc.sync.dma_start(out=w1_rows[:], in_=W1.rearrange("(q t) h -> q t h", t=PACK))
            x_rows[i] = keep.tile([P, PACK, FEATURES], BF16, name="x_rows%d" % i)
            step = 2 if i == 0 else PACK
            for j in range(0, PACK, step):
                nc.sync.dma_start(
                    out=x_rows[i][:, j : j + step, :],
                    in_=x_view[i // NODE_PASSES, i % NODE_PASSES, :, j : j + step, :],
                )
        adj_view = adj.rearrange("(p t) m -> p t m", t=NODE_TILES)
        s_view = S.rearrange("(p t) m -> p t m", t=NODE_TILES)
        out_view = out.rearrange("b (p t) h -> b p t h", t=NODE_TILES)
        adj_rows = []
        s_rows = []
        for r in range(PAIRS):
            a = keep.tile([P, 2, NODES], BF16, name="adj_rows%d" % r)
            nc.sync.dma_start(out=a[:], in_=adj_view[:, 2 * r : 2 * r + 2, :])
            adj_rows.append(a)
            s = keep.tile([P, 2, NODES], BF16, name="s_rows%d" % r)
            nc.sync.dma_start(out=s[:], in_=s_view[:, 2 * r : 2 * r + 2, :])
            s_rows.append(s)

        ident = keep.tile([P, P], F32, name="ident")
        make_identity(nc, ident[:])

        zeros = keep.tile([P, HIDDEN], BF16, name="zeros")
        nc.vector.memset(zeros[:], 0.0)
        idle_bank = mm_psum.tile([P, HIDDEN], F32, tag="mm", name="idle_bank")

        def keep_busy(count):
            for i in range(count):
                nc.tensor.matmul(out=idle_bank[:], lhsT=zeros[:, :P], rhs=zeros[:], start=True, stop=True)

        w1_grouped = keep.tile([P, HIDDEN, PACK], BF16, name="w1_grouped", align_bytes=64)
        w1_codes = keep.tile([P, HIDDEN], U32, name="w1_codes", align_bytes=64)
        w1_scales = keep.tile([P, HIDDEN], U8, name="w1_scales", align_bytes=64)

        def regroup_w1(half):
            cols = slice(half * HIDDEN // 2, (half + 1) * HIDDEN // 2)
            nc.vector.tensor_copy(
                out=w1_grouped[:, cols, :].rearrange("q (c i) t -> q c t i", i=4),
                in_=w1_rows[:, :, cols].rearrange("q t (c i) -> q c t i", i=4),
            )

        def quantise_w1(half):
            cols = slice(half * HIDDEN // 2, (half + 1) * HIDDEN // 2)
            nc.vector.quantize_mx(
                out=w1_codes[:, cols].bitcast(FP8X4),
                scales=w1_scales[:, cols],
                in_=w1_grouped[:, cols, :].rearrange("q h t -> q (h t)"),
            )

        def quantise(name, grouped):
            codes = keep.tile([P, K_PASS], U32, name=name + "_codes", align_bytes=64)
            scales = keep.tile([P, K_PASS], U8, name=name + "_scales", align_bytes=64)
            nc.vector.quantize_mx(out=codes[:].bitcast(FP8X4), scales=scales[:], in_=grouped)
            return codes, scales

        def transpose_words(blocks):
            bank = tr_psum.tile([P, PACK, P], F32, tag="tr", name="tr_bank")
            for c, block in enumerate(blocks):
                nc.tensor.transpose(bank[:, c, :], block, ident[:])
            return bank

        x_banks = {}
        x_grouped = {}
        x_q = {}
        sup_banks = {}
        sup_grouped = {}
        sup_q = {}

        def transpose_x(i):
            x_banks[i] = []
            for u in range(2):
                words = x_rows[i][:, 2 * u : 2 * u + 2, :].bitcast(F32)
                x_banks[i].append(
                    transpose_words([words[:, e, uk : uk + 2 * P - 1 : 2] for e in range(2) for uk in range(2)])
                )

        def copy_x(i):
            x_grouped[i] = keep.tile([P, PACK, P, PACK], BF16, name="x_grouped%d" % i, align_bytes=64)
            for u in range(2):
                nc.scalar.copy(
                    out=x_grouped[i][:, 2 * u : 2 * u + 2, :, :].bitcast(F32),
                    in_=x_banks[i][u][:].rearrange("q (e uk) m -> q e m uk", e=2),
                )

        def quantise_x(i):
            x_q[i] = quantise("x%d" % i, x_grouped[i][:].rearrange("q j m t -> q (j m t)"))

        def support_matmuls(i):
            codes, scales = x_q[i]
            sup_banks[i] = []
            for hq in range(QUARTERS):
                h_cols = slice(hq * P, (hq + 1) * P)
                bank = mm_psum.tile([P, PACK, P], F32, tag="mm", name="sup_bank")
                for j in range(PACK):
                    m_cols = slice(j * P, (j + 1) * P)
                    nc.tensor.matmul_mx(
                        out=bank[:, j, :],
                        lhsT=codes[:, m_cols].bitcast(FP8X4),
                        lhsT_scale=scales[:, m_cols],
                        rhs=w1_codes[:, h_cols].bitcast(FP8X4),
                        rhs_scale=w1_scales[:, h_cols],
                        start=True,
                        stop=True,
                    )
                sup_banks[i].append(bank)

        def copy_support(i):
            sup_grouped[i] = keep.tile([P, HIDDEN, PACK], BF16, name="sup_grouped%d" % i, align_bytes=64)
            on_vector = {0: (1, 3), 1: (3,)}.get(i, ())
            for hq in range(QUARTERS):
                dst = sup_grouped[i][:, hq * P : (hq + 1) * P, :]
                src = sup_banks[i][hq][:].rearrange("p j h -> p h j")
                if hq in on_vector:
                    nc.vector.tensor_copy(out=dst, in_=src)
                else:
                    nc.scalar.copy(out=dst, in_=src)

        def quantise_support(i):
            sup_q[i] = quantise("sup%d" % i, sup_grouped[i][:].rearrange("p h j -> p (h j)"))

        w_rows = {}
        w_banks = {}
        w_grouped = {}
        w_q = {}
        out_banks = {}

        def product(r):
            w_rows[r] = keep.tile([P, 2, NODES // 2, 2], BF16, name="w_rows%d" % r)
            pairs = "p t (gq u e) -> p u (t gq) e"
            nc.vector.tensor_tensor(
                out=w_rows[r][:],
                in0=adj_rows[r][:].rearrange(pairs, u=2, e=2),
                in1=s_rows[r][:].rearrange(pairs, u=2, e=2),
                op=mybir.AluOpType.mult,
            )

        def transpose_w(r):
            words = w_rows[r][:].rearrange("p u n e -> p (u n e)").bitcast(F32)
            w_banks[r] = []
            for t in range(2):
                firsts = [(2 * NODE_PASSES * u + NODE_PASSES * t + g) * P for g in range(NODE_PASSES) for u in range(2)]
                w_banks[r].append(transpose_words([words[:, first : first + P] for first in firsts]))

        def copy_w(r):
            w_grouped[r] = keep.tile([P, 2, NODE_PASSES, P, PACK], BF16, name="w_grouped%d" % r, align_bytes=64)
            for t in range(2):
                dst = w_grouped[r][:, t, :, :, :].bitcast(F32)
                src = w_banks[r][t][:].rearrange("p (g u) n -> p g n u", g=NODE_PASSES)
                if r > 0 and t == 0:
                    nc.vector.tensor_copy(out=dst, in_=src)
                else:
                    nc.scalar.copy(out=dst, in_=src)

        def quantise_w(r):
            w_q[r] = quantise("w%d" % r, w_grouped[r][:].rearrange("p t g n v -> p (t g n v)"))

        def output_matmuls(r, b):
            codes, scales = w_q[r]
            for t in range(2):
                bank = mm_psum.tile([P, HIDDEN], F32, tag="mm", name="out_bank")
                for g in range(NODE_PASSES):
                    n_cols = slice((t * NODE_PASSES + g) * P, (t * NODE_PASSES + g + 1) * P)
                    s_codes, s_scales = sup_q[b * NODE_PASSES + g]
                    nc.tensor.matmul_mx(
                        out=bank[:],
                        lhsT=codes[:, n_cols].bitcast(FP8X4),
                        lhsT_scale=scales[:, n_cols],
                        rhs=s_codes[:].bitcast(FP8X4),
                        rhs_scale=s_scales[:],
                        start=(g == 0),
                        stop=(g == NODE_PASSES - 1),
                    )
                out_banks[(r, b, t)] = bank

        def relu_and_store(r, b):
            for t in range(2):
                result = keep.tile([P, HIDDEN], F32, name="result%d_%d_%d" % (r, b, t))
                if t == 1 and r > 0:
                    nc.vector.tensor_scalar_max(out=result[:], in0=out_banks[(r, b, t)][:], scalar1=0.0)
                else:
                    nc.scalar.activation(
                        out=result[:], in_=out_banks[(r, b, t)][:], func=mybir.ActivationFunctionType.Relu
                    )
                nc.sync.dma_start(out=out_view[b, :, 2 * r + t, :], in_=result[:])

        keep_busy(4)
        transpose_x(0)
        keep_busy(2)
        copy_x(0)
        regroup_w1(0)
        quantise_x(0)
        quantise_w1(0)
        regroup_w1(1)
        quantise_w1(1)
        transpose_x(1)
        keep_busy(2)
        copy_x(1)
        transpose_x(2)
        copy_x(2)
        quantise_x(1)
        support_matmuls(0)
        copy_support(0)
        quantise_x(2)
        support_matmuls(1)
        transpose_x(3)
        product(0)
        transpose_w(0)
        quantise_support(0)
        copy_support(1)
        copy_x(3)
        copy_w(0)
        product(1)
        support_matmuls(2)
        quantise_x(3)
        transpose_w(1)
        quantise_w(0)
        copy_support(2)
        support_matmuls(3)
        product(2)
        transpose_w(2)
        quantise_support(1)
        copy_w(1)
        copy_support(3)
        product(3)
        output_matmuls(0, 0)
        quantise_w(1)
        quantise_support(2)
        transpose_w(3)
        relu_and_store(0, 0)
        output_matmuls(1, 0)
        quantise_support(3)
        copy_w(2)
        relu_and_store(1, 0)
        output_matmuls(0, 1)
        quantise_w(2)
        relu_and_store(0, 1)
        output_matmuls(1, 1)
        copy_w(3)
        relu_and_store(1, 1)
        quantise_w(3)
        output_matmuls(2, 0)
        output_matmuls(2, 1)
        relu_and_store(2, 0)
        relu_and_store(2, 1)
        output_matmuls(3, 0)
        output_matmuls(3, 1)
        relu_and_store(3, 0)
        relu_and_store(3, 1)
